import numpy as np
import ml_dtypes


def mxq(x, axis, fmt="e4m3"):
    dtype, down = {"e4m3": (ml_dtypes.float8_e4m3fn, 7), "e5m2": (ml_dtypes.float8_e5m2, 14)}[fmt]
    v = np.moveaxis(np.asarray(x, np.float32).astype(ml_dtypes.bfloat16).astype(np.float64), axis, -1)
    blocks = v.reshape(v.shape[:-1] + (-1, 32))
    amax = np.abs(blocks).max(-1, keepdims=True)
    byte = np.maximum(np.where(amax > 0, np.frexp(amax)[1] - 1 + 127, 0) - down, 1)
    scale = np.exp2(byte - 127.0)
    codes = (blocks / scale).astype(np.float32).astype(dtype).astype(np.float64)
    return np.moveaxis((codes * scale).reshape(v.shape), -1, axis)


WIDE = False


def mx_kscale(k):
    if not WIDE:
        return np.ones(k)
    levels = np.array([10, -10, 5, -5, 0])
    a = np.random.permutation(np.resize(levels, k // 512 * 4)).reshape(k // 512, 4)
    idx = np.arange(k)
    return np.exp2(a[idx // 512, idx % 128 // 32])


BF16 = ml_dtypes.bfloat16


def bf(x):
    return np.asarray(x, np.float32).astype(BF16)


def f64(x):
    return np.asarray(x).astype(np.float64)


B, S, H, O, W = 8, 128, 1024, 2048, 8


def setup_inputs():
    s = mx_kscale(H)
    return {"hidden_states": bf(np.random.standard_normal((B, S, H)) * s),
            "gate_proj": bf(np.random.standard_normal((O, H)) / np.sqrt(H) / s[None, :]),
            "world_size": W}


def reference(hidden_states, gate_proj, world_size):
    h = gate_proj.shape[1]
    view = f64(hidden_states).reshape(-1, h)
    mm = mxq(view, 1, "e4m3") @ mxq(f64(gate_proj), 1, "e4m3").T
    n, o = mm.shape
    out = mm.reshape(world_size, n // world_size, o).sum(axis=0)
    return out

@@ -1,0 +1,204 @@
+from contextlib import ExitStack
+
+import concourse.mybir as mybir
+from concourse.masks import make_identity
+
+F32 = mybir.dt.float32
+BF16 = mybir.dt.bfloat16
+U32 = mybir.dt.uint32
+U8 = mybir.dt.uint8
+FP8X4 = mybir.dt.float8_e4m3fn_x4
+
+P = 128
+R = 8
+K = 1024
+O = 2048
+G = K // 512
+NCH = 4
+T = 4
+
+FLOPS = 2 * R * P * K * O
+
+
+def tile_testmmrsmodel_kernel(tc, hidden_states, gate_proj, world_size, out):
+    nc = tc.nc
+    assert world_size == R
+    with ExitStack() as ctx:
+        keep = ctx.enter_context(tc.tile_pool(name="keep", bufs=1))
+        tp = ctx.enter_context(tc.psum_pool(name="tp", bufs=6))
+        accp = ctx.enter_context(tc.psum_pool(name="accp", bufs=2))
+        ctx.enter_context(tc.manual_schedule())
+
+        ident = keep.tile([P, P], F32, name="ident")
+        x_raw = keep.tile([P, R * K], BF16, name="x_raw")
+        x_grp = keep.tile([P, R * K], BF16, name="x_grp", align_bytes=64)
+        x_codes = keep.tile([P, R * K // 4], U32, name="x_codes", align_bytes=64)
+        x_scales = keep.tile([P, R * K // 4], U8, name="x_scales", align_bytes=64)
+        w_raw = [keep.tile([P, T * K], BF16, name="w_raw%d" % n) for n in range(NCH)]
+        w_grp = [
+            keep.tile([P, T * K], BF16, name="w_grp%d" % n, align_bytes=64)
+            for n in range(NCH)
+        ]
+        w_codes = [
+            keep.tile([P, T * K // 4], U32, name="w_codes%d" % n, align_bytes=64)
+            for n in range(NCH)
+        ]
+        w_scales = [
+            keep.tile([P, T * K // 4], U8, name="w_scales%d" % n, align_bytes=64)
+            for n in range(NCH)
+        ]
+        out_sb = [keep.tile([P, 512], F32, name="out_sb%d" % n) for n in range(NCH)]
+
+        w_view = gate_proj.rearrange("(n p t) k -> n p (t k)", n=NCH, p=P)
+        half = T * K // 2
+        nc.sync.dma_start(out=w_raw[0][:, 0:half], in_=w_view[0, :, 0:half])
+        nc.sync.dma_start(out=w_raw[0][:, half:], in_=w_view[0, :, half:])
+        for r in range(R):
+            nc.sync.dma_start(out=x_raw[:, r * K : (r + 1) * K], in_=hidden_states[r])
+        for n in range(1, NCH):
+            nc.sync.dma_start(out=w_raw[n][:], in_=w_view[n])
+
+        make_identity(nc, ident[:])
+
+        x_words = x_raw[:].bitcast(F32)
+        x_grp32 = x_grp[:].bitcast(F32)
+        w_words = [w_raw[n][:].bitcast(F32) for n in range(NCH)]
+        w_grp32 = [
+            w_grp[n][:].bitcast(F32).rearrange(
+                "q (g t r u) -> q g t r u", g=G, t=T, u=2
+            )
+            for n in range(NCH)
+        ]
+
+        def transpose_unit(words):
+            bank = tp.tile([P, 4, P], F32, name="bank", tag="bank")
+            for c in range(4):
+                nc.tensor.transpose(
+                    bank[:, c, :], words[:, c * P : (c + 1) * P], ident[:]
+                )
+            return bank
+
+        def t_x(r):
+            return transpose_unit(x_words[:, 512 * r : 512 * (r + 1)])
+
+        def t_w(n, t):
+            return transpose_unit(w_words[n][:, 512 * t : 512 * (t + 1)])
+
+        def c_x(copy, bank, r):
+            copy(
+                out=x_grp32[:, 512 * r : 512 * (r + 1)].rearrange(
+                    "q (g r u) -> q g r u", g=G, u=2
+                ),
+                in_=bank[:].rearrange("q (g u) r -> q g r u", u=2),
+            )
+
+        def c_w(copy, bank, n, t):
+            copy(
+                out=w_grp32[n][:, :, t, :, :],
+                in_=bank[:].rearrange("q (g u) r -> q g r u", u=2),
+            )
+
+        def q_x(r):
+            nc.vector.quantize_mx(
+                out=x_codes[:, 256 * r : 256 * (r + 1)].bitcast(FP8X4),
+                scales=x_scales[:, 256 * r : 256 * (r + 1)],
+                in_=x_grp[:, 1024 * r : 1024 * (r + 1)],
+            )
+
+        def q_w(n, first, count):
+            nc.vector.quantize_mx(
+                out=w_codes[n][:, first : first + count].bitcast(FP8X4),
+                scales=w_scales[n][:, first : first + count],
+                in_=w_grp[n][:, 4 * first : 4 * (first + count)],
+            )
+
+        def mx(acc, n, r, g, start, stop):
+            xs = slice(256 * r + 128 * g, 256 * r + 128 * (g + 1))
+            ws = slice(512 * g, 512 * (g + 1))
+            nc.tensor.matmul_mx(
+                out=acc[:],
+                lhsT=x_codes[:, xs].bitcast(FP8X4),
+                lhsT_scale=x_scales[:, xs],
+                rhs=w_codes[n][:, ws].bitcast(FP8X4),
+                rhs_scale=w_scales[n][:, ws],
+                start=start,
+                stop=stop,
+            )
+
+        def finish(copy, acc, n):
+            copy(
+                out=out_sb[n][:].rearrange("j (p t) -> j p t", t=T),
+                in_=acc[:].rearrange("j (t p) -> j p t", t=T),
+            )
+            nc.sync.dma_start(out=out[:, 512 * n : 512 * (n + 1)], in_=out_sb[n][:])
+
+        s_copy = nc.scalar.copy
+        v_copy = nc.vector.tensor_copy
+
+        b0 = t_w(0, 0)
+        b1 = t_w(0, 1)
+        c_w(s_copy, b0, 0, 0)
+        c_w(v_copy, b1, 0, 1)
+        b2 = t_w(0, 2)
+        b3 = t_w(0, 3)
+        q_w(0, 0, 128)
+        q_w(0, 512, 128)
+        c_w(s_copy, b2, 0, 2)
+        q_w(0, 128, 128)
+        q_w(0, 640, 128)
+        c_w(v_copy, b3, 0, 3)
+        bx = t_x(0)
+        c_x(s_copy, bx, 0)
+        q_w(0, 256, 128)
+        q_w(0, 768, 128)
+        bx = t_x(1)
+        c_x(s_copy, bx, 1)
+        q_w(0, 384, 128)
+        q_w(0, 896, 128)
+        q_x(0)
+        bx = t_x(2)
+        c_x(s_copy, bx, 2)
+        q_x(1)
+        bx = t_x(3)
+        c_x(s_copy, bx, 3)
+
+        acc = accp.tile([P, 512], F32, name="acc", tag="acc")
+
+        def mx_pair(first):
+            for r in (first, first + 1):
+                for g in range(G):
+                    mx(acc, 0, r, g, r == 0 and g == 0, r == R - 1 and g == G - 1)
+
+        for first in (4, 6):
+            mx_pair(first - 4)
+            q_x(first - 2)
+            q_x(first - 1)
+            for r in (first, first + 1):
+                bx = t_x(r)
+                c_x(s_copy, bx, r)
+        mx_pair(4)
+        q_x(6)
+        q_x(7)
+
+        def prepare(n):
+            banks = [t_w(n, t) for t in range(T)]
+            for t in range(T):
+                c_w(v_copy if t % 2 == 0 else s_copy, banks[t], n, t)
+
+        prepare(1)
+        mx_pair(6)
+        q_w(1, 0, 512)
+        q_w(1, 512, 512)
+        finish(s_copy, acc, 0)
+
+        for n in range(1, NCH):
+            if n + 1 < NCH:
+                prepare(n + 1)
+            acc = accp.tile([P, 512], F32, name="acc", tag="acc")
+            for g in range(G):
+                for r in range(R):
+                    mx(acc, n, r, g, g == 0 and r == 0, g == G - 1 and r == R - 1)
+            if n + 1 < NCH:
+                q_w(n + 1, 0, 512)
+                q_w(n + 1, 512, 512)
+            finish(s_copy if n + 1 < NCH else v_copy, acc, n)

@@ -17,6 +17,8 @@ G = K // 512
 NCH = 4
 T = 4
 
+WARM_START = 8
+
 FLOPS = 2 * R * P * K * O
 
 
@@ -59,6 +61,18 @@ def tile_testmmrsmodel_kernel(tc, hidden_states, gate_proj, world_size, out):
             nc.sync.dma_start(out=w_raw[n][:], in_=w_view[n])
 
         make_identity(nc, ident[:])
+
+        zeros = keep.tile([P, 512], BF16, name="zeros")
+        nc.vector.memset(zeros[:], 0.0)
+        warm = accp.tile([P, 512], F32, name="warm", tag="acc")
+
+        def dummy(count):
+            for i in range(count):
+                nc.tensor.matmul(
+                    out=warm[:], lhsT=zeros[:, 0:P], rhs=zeros[:], start=True, stop=True
+                )
+
+        dummy(WARM_START)
 
         x_words = x_raw[:].bitcast(F32)
         x_grp32 = x_grp[:].bitcast(F32)
@@ -137,10 +151,12 @@ def tile_testmmrsmodel_kernel(tc, hidden_states, gate_proj, world_size, out):
 
         b0 = t_w(0, 0)
         b1 = t_w(0, 1)
+        dummy(1)
         c_w(s_copy, b0, 0, 0)
         c_w(v_copy, b1, 0, 1)
         b2 = t_w(0, 2)
         b3 = t_w(0, 3)
+        dummy(1)
         q_w(0, 0, 128)
         q_w(0, 512, 128)
         c_w(s_copy, b2, 0, 2)
@@ -152,6 +168,7 @@ def tile_testmmrsmodel_kernel(tc, hidden_states, gate_proj, world_size, out):
         q_w(0, 256, 128)
         q_w(0, 768, 128)
         bx = t_x(1)
+        dummy(1)
         c_x(s_copy, bx, 1)
         q_w(0, 384, 128)
         q_w(0, 896, 128)

@@ -16,8 +16,7 @@ O = 2048
 G = K // 512
 NCH = 4
 T = 4
-
-WARM_START = 8
+LAST = NCH - 1
 
 FLOPS = 2 * R * P * K * O
 
@@ -51,28 +50,33 @@ def tile_testmmrsmodel_kernel(tc, hidden_states, gate_proj, world_size, out):
         ]
         out_sb = [keep.tile([P, 512], F32, name="out_sb%d" % n) for n in range(NCH)]
 
-        w_view = gate_proj.rearrange("(n p t) k -> n p (t k)", n=NCH, p=P)
         half = T * K // 2
-        nc.sync.dma_start(out=w_raw[0][:, 0:half], in_=w_view[0, :, 0:half])
-        nc.sync.dma_start(out=w_raw[0][:, half:], in_=w_view[0, :, half:])
+
+        def load_w_halves(n):
+            view = gate_proj[512 * n : 512 * (n + 1), :].rearrange(
+                "(p t) k -> p (t k)", t=T
+            )
+            nc.sync.dma_start(out=w_raw[n][:, 0:half], in_=view[:, 0:half])
+            nc.sync.dma_start(out=w_raw[n][:, half:], in_=view[:, half:])
+
+        load_w_halves(0)
         for r in range(R):
             nc.sync.dma_start(out=x_raw[:, r * K : (r + 1) * K], in_=hidden_states[r])
-        for n in range(1, NCH):
-            nc.sync.dma_start(out=w_raw[n][:], in_=w_view[n])
+        nc.sync.dma_start(
+            out=w_raw[1][:],
+            in_=gate_proj[512:1024, :].rearrange("(p t) k -> p (t k)", t=T),
+        )
+        load_w_halves(2)
+        for h in range(2):
+            first_row = 512 * LAST + 256 * h
+            nc.sync.dma_start(
+                out=w_raw[LAST][:, h * half : (h + 1) * half],
+                in_=gate_proj[first_row : first_row + 256, :].rearrange(
+                    "(p t) k -> p (t k)", t=2
+                ),
+            )
 
         make_identity(nc, ident[:])
-
-        zeros = keep.tile([P, 512], BF16, name="zeros")
-        nc.vector.memset(zeros[:], 0.0)
-        warm = accp.tile([P, 512], F32, name="warm", tag="acc")
-
-        def dummy(count):
-            for i in range(count):
-                nc.tensor.matmul(
-                    out=warm[:], lhsT=zeros[:, 0:P], rhs=zeros[:], start=True, stop=True
-                )
-
-        dummy(WARM_START)
 
         x_words = x_raw[:].bitcast(F32)
         x_grp32 = x_grp[:].bitcast(F32)
@@ -81,8 +85,11 @@ def tile_testmmrsmodel_kernel(tc, hidden_states, gate_proj, world_size, out):
             w_grp[n][:].bitcast(F32).rearrange(
                 "q (g t r u) -> q g t r u", g=G, t=T, u=2
             )
-            for n in range(NCH)
+            for n in range(LAST)
         ]
+        w_grp32_last = w_grp[LAST][:].bitcast(F32).rearrange(
+            "q (h g t r u) -> q h g t r u", h=2, g=G, t=2, u=2
+        )
 
         def transpose_unit(words):
             bank = tp.tile([P, 4, P], F32, name="bank", tag="bank")
@@ -107,10 +114,11 @@ def tile_testmmrsmodel_kernel(tc, hidden_states, gate_proj, world_size, out):
             )
 
         def c_w(copy, bank, n, t):
-            copy(
-                out=w_grp32[n][:, :, t, :, :],
-                in_=bank[:].rearrange("q (g u) r -> q g r u", u=2),
-            )
+            if n < LAST:
+                dst = w_grp32[n][:, :, t, :, :]
+            else:
+                dst = w_grp32_last[:, t // 2, :, t % 2, :, :]
+            copy(out=dst, in_=bank[:].rearrange("q (g u) r -> q g r u", u=2))
 
         def q_x(r):
             nc.vector.quantize_mx(
@@ -126,9 +134,9 @@ def tile_testmmrsmodel_kernel(tc, hidden_states, gate_proj, world_size, out):
                 in_=w_grp[n][:, 4 * first : 4 * (first + count)],
             )
 
-        def mx(acc, n, r, g, start, stop):
+        def mx(acc, n, first, count, r, g, start, stop):
             xs = slice(256 * r + 128 * g, 256 * r + 128 * (g + 1))
-            ws = slice(512 * g, 512 * (g + 1))
+            ws = slice(first, first + count)
             nc.tensor.matmul_mx(
                 out=acc[:],
                 lhsT=x_codes[:, xs].bitcast(FP8X4),
@@ -139,24 +147,23 @@ def tile_testmmrsmodel_kernel(tc, hidden_states, gate_proj, world_size, out):
                 stop=stop,
             )
 
-        def finish(copy, acc, n):
+        def finish(copy, acc, first_col, count, dst):
+            rows = count // P
             copy(
-                out=out_sb[n][:].rearrange("j (p t) -> j p t", t=T),
-                in_=acc[:].rearrange("j (t p) -> j p t", t=T),
+                out=dst.rearrange("j (p t) -> j p t", t=rows),
+                in_=acc[:].rearrange("j (t p) -> j p t", t=rows),
             )
-            nc.sync.dma_start(out=out[:, 512 * n : 512 * (n + 1)], in_=out_sb[n][:])
+            nc.sync.dma_start(out=out[:, first_col : first_col + count], in_=dst)
 
         s_copy = nc.scalar.copy
         v_copy = nc.vector.tensor_copy
 
         b0 = t_w(0, 0)
         b1 = t_w(0, 1)
-        dummy(1)
         c_w(s_copy, b0, 0, 0)
         c_w(v_copy, b1, 0, 1)
         b2 = t_w(0, 2)
         b3 = t_w(0, 3)
-        dummy(1)
         q_w(0, 0, 128)
         q_w(0, 512, 128)
         c_w(s_copy, b2, 0, 2)
@@ -168,7 +175,6 @@ def tile_testmmrsmodel_kernel(tc, hidden_states, gate_proj, world_size, out):
         q_w(0, 256, 128)
         q_w(0, 768, 128)
         bx = t_x(1)
-        dummy(1)
         c_x(s_copy, bx, 1)
         q_w(0, 384, 128)
         q_w(0, 896, 128)
@@ -179,43 +185,77 @@ def tile_testmmrsmodel_kernel(tc, hidden_states, gate_proj, world_size, out):
         bx = t_x(3)
         c_x(s_copy, bx, 3)
 
-        acc = accp.tile([P, 512], F32, name="acc", tag="acc")
+        acc0 = accp.tile([P, 512], F32, name="acc0", tag="acc")
 
-        def mx_pair(first):
-            for r in (first, first + 1):
+        def mx_rows(rows):
+            for r in rows:
                 for g in range(G):
-                    mx(acc, 0, r, g, r == 0 and g == 0, r == R - 1 and g == G - 1)
+                    mx(
+                        acc0, 0, 512 * g, 512, r, g,
+                        r == 0 and g == 0, r == R - 1 and g == G - 1,
+                    )
 
-        for first in (4, 6):
-            mx_pair(first - 4)
-            q_x(first - 2)
-            q_x(first - 1)
-            for r in (first, first + 1):
-                bx = t_x(r)
-                c_x(s_copy, bx, r)
-        mx_pair(4)
+        mx_rows((0, 1))
+        q_x(2)
+        q_x(3)
+        bxs = [t_x(r) for r in range(4, 8)]
+        c_x(s_copy, bxs[0], 4)
+        c_x(v_copy, bxs[1], 5)
+        q_x(4)
+        c_x(s_copy, bxs[2], 6)
+        c_x(v_copy, bxs[3], 7)
+        q_x(5)
         q_x(6)
         q_x(7)
+        mx_rows((2, 3, 4, 5))
 
-        def prepare(n):
-            banks = [t_w(n, t) for t in range(T)]
-            for t in range(T):
-                c_w(v_copy if t % 2 == 0 else s_copy, banks[t], n, t)
-
-        prepare(1)
-        mx_pair(6)
+        bw1 = [t_w(1, t) for t in range(T)]
+        bw2 = [t_w(2, t) for t in range(2)]
+        c_w(v_copy, bw1[0], 1, 0)
+        c_w(s_copy, bw1[1], 1, 1)
+        c_w(v_copy, bw1[2], 1, 2)
+        c_w(s_copy, bw1[3], 1, 3)
         q_w(1, 0, 512)
         q_w(1, 512, 512)
-        finish(s_copy, acc, 0)
+        c_w(s_copy, bw2[1], 2, 1)
+        c_w(v_copy, bw2[0], 2, 0)
+        mx_rows((6, 7))
+        finish(s_copy, acc0, 0, 512, out_sb[0][:])
+        q_w(2, 0, 256)
+        q_w(2, 512, 256)
 
-        for n in range(1, NCH):
-            if n + 1 < NCH:
-                prepare(n + 1)
-            acc = accp.tile([P, 512], F32, name="acc", tag="acc")
+        def mx_chunk(acc, n, first, count):
             for g in range(G):
                 for r in range(R):
-                    mx(acc, n, r, g, g == 0 and r == 0, g == G - 1 and r == R - 1)
-            if n + 1 < NCH:
-                q_w(n + 1, 0, 512)
-                q_w(n + 1, 512, 512)
-            finish(s_copy if n + 1 < NCH else v_copy, acc, n)
+                    mx(
+                        acc, n, first + count * g, count, r, g,
+                        g == 0 and r == 0, g == G - 1 and r == R - 1,
+                    )
+
+        acc1 = accp.tile([P, 512], F32, name="acc1", tag="acc")
+        mx_chunk(acc1, 1, 0, 512)
+
+        bw2 = [t_w(2, t) for t in range(2, T)]
+        bw3 = [t_w(LAST, t) for t in range(T)]
+        finish(s_copy, acc1, 512, 512, out_sb[1][:])
+        c_w(v_copy, bw2[0], 2, 2)
+        c_w(s_copy, bw2[1], 2, 3)
+        q_w(2, 256, 256)
+        q_w(2, 768, 256)
+        c_w(v_copy, bw3[0], LAST, 0)
+        c_w(s_copy, bw3[1], LAST, 1)
+        c_w(v_copy, bw3[2], LAST, 2)
+        c_w(s_copy, bw3[3], LAST, 3)
+
+        acc2 = accp.tile([P, 512], F32, name="acc2", tag="acc")
+        mx_chunk(acc2, 2, 0, 512)
+        q_w(LAST, 0, 512)
+        q_w(LAST, 512, 512)
+        finish(s_copy, acc2, 1024, 512, out_sb[2][:])
+
+        acc3a = accp.tile([P, 256], F32, name="acc3a", tag="acc")
+        mx_chunk(acc3a, LAST, 0, 256)
+        finish(s_copy, acc3a, 1536, 256, out_sb[LAST][:, 0:256])
+        acc3b = accp.tile([P, 256], F32, name="acc3b", tag="acc")
+        mx_chunk(acc3b, LAST, 512, 256)
+        finish(v_copy, acc3b, 1792, 256, out_sb[LAST][:, 256:512])

@@ -35,7 +35,10 @@ def tile_testmmrsmodel_kernel(tc, hidden_states, gate_proj, world_size, out):
         x_grp = keep.tile([P, R * K], BF16, name="x_grp", align_bytes=64)
         x_codes = keep.tile([P, R * K // 4], U32, name="x_codes", align_bytes=64)
         x_scales = keep.tile([P, R * K // 4], U8, name="x_scales", align_bytes=64)
-        w_raw = [keep.tile([P, T * K], BF16, name="w_raw%d" % n) for n in range(NCH)]
+        w_raw = [
+            keep.tile([P, T * K], BF16, name="w_raw%d" % n, align_bytes=64)
+            for n in range(NCH)
+        ]
         w_grp = [
             keep.tile([P, T * K], BF16, name="w_grp%d" % n, align_bytes=64)
             for n in range(NCH)
@@ -67,14 +70,18 @@ def tile_testmmrsmodel_kernel(tc, hidden_states, gate_proj, world_size, out):
             in_=gate_proj[512:1024, :].rearrange("(p t) k -> p (t k)", t=T),
         )
         load_w_halves(2)
-        for h in range(2):
-            first_row = 512 * LAST + 256 * h
-            nc.sync.dma_start(
-                out=w_raw[LAST][:, h * half : (h + 1) * half],
-                in_=gate_proj[first_row : first_row + 256, :].rearrange(
-                    "(p t) k -> p (t k)", t=2
-                ),
-            )
+        for g in range(G):
+            for a in range(4):
+                for u in range(2):
+                    k0 = 512 * g + 256 * u + 64 * a
+                    nc.sync.dma_start(
+                        out=w_raw[LAST][
+                            32 * a + u : 32 * (a + 1) : 2, half * g : half * (g + 1)
+                        ].rearrange("m (b k) -> m b k", k=64),
+                        in_=gate_proj[512 * LAST : O, k0 : k0 + 64].rearrange(
+                            "(m b) k -> m b k", b=32
+                        ),
+                    )
 
         make_identity(nc, ident[:])
 
@@ -87,9 +94,7 @@ def tile_testmmrsmodel_kernel(tc, hidden_states, gate_proj, world_size, out):
             )
             for n in range(LAST)
         ]
-        w_grp32_last = w_grp[LAST][:].bitcast(F32).rearrange(
-            "q (h g t r u) -> q h g t r u", h=2, g=G, t=2, u=2
-        )
+        w_grp32_last = w_grp[LAST][:].bitcast(F32)
 
         def transpose_unit(words):
             bank = tp.tile([P, 4, P], F32, name="bank", tag="bank")
@@ -114,11 +119,16 @@ def tile_testmmrsmodel_kernel(tc, hidden_states, gate_proj, world_size, out):
             )
 
         def c_w(copy, bank, n, t):
-            if n < LAST:
-                dst = w_grp32[n][:, :, t, :, :]
-            else:
-                dst = w_grp32_last[:, t // 2, :, t % 2, :, :]
-            copy(out=dst, in_=bank[:].rearrange("q (g u) r -> q g r u", u=2))
+            copy(
+                out=w_grp32[n][:, :, t, :, :],
+                in_=bank[:].rearrange("q (g u) r -> q g r u", u=2),
+            )
+
+        def vt_last(g):
+            nc.vector.transpose(
+                out=w_grp32_last[:, 1024 * g : 1024 * (g + 1)],
+                in_=w_words[LAST][:, 1024 * g : 1024 * (g + 1)],
+            )
 
         def q_x(r):
             nc.vector.quantize_mx(
@@ -224,38 +234,41 @@ def tile_testmmrsmodel_kernel(tc, hidden_states, gate_proj, world_size, out):
         q_w(2, 0, 256)
         q_w(2, 512, 256)
 
-        def mx_chunk(acc, n, first, count):
-            for g in range(G):
-                for r in range(R):
-                    mx(
-                        acc, n, first + count * g, count, r, g,
-                        g == 0 and r == 0, g == G - 1 and r == R - 1,
-                    )
+        def mx_part(acc, n, first, count, g):
+            for r in range(R):
+                mx(
+                    acc, n, first, count, r, g,
+                    g == 0 and r == 0, g == G - 1 and r == R - 1,
+                )
 
         acc1 = accp.tile([P, 512], F32, name="acc1", tag="acc")
-        mx_chunk(acc1, 1, 0, 512)
-
+        mx_part(acc1, 1, 0, 512, 0)
         bw2 = [t_w(2, t) for t in range(2, T)]
-        bw3 = [t_w(LAST, t) for t in range(T)]
-        finish(s_copy, acc1, 512, 512, out_sb[1][:])
         c_w(v_copy, bw2[0], 2, 2)
         c_w(s_copy, bw2[1], 2, 3)
         q_w(2, 256, 256)
         q_w(2, 768, 256)
-        c_w(v_copy, bw3[0], LAST, 0)
-        c_w(s_copy, bw3[1], LAST, 1)
-        c_w(v_copy, bw3[2], LAST, 2)
-        c_w(s_copy, bw3[3], LAST, 3)
+        mx_part(acc1, 1, 512, 512, 1)
+        finish(s_copy, acc1, 512, 512, out_sb[1][:])
 
         acc2 = accp.tile([P, 512], F32, name="acc2", tag="acc")
-        mx_chunk(acc2, 2, 0, 512)
-        q_w(LAST, 0, 512)
-        q_w(LAST, 512, 512)
+        mx_part(acc2, 2, 0, 512, 0)
+        mx_part(acc2, 2, 512, 512, 1)
         finish(s_copy, acc2, 1024, 512, out_sb[2][:])
 
-        acc3a = accp.tile([P, 256], F32, name="acc3a", tag="acc")
-        mx_chunk(acc3a, LAST, 0, 256)
-        finish(s_copy, acc3a, 1536, 256, out_sb[LAST][:, 0:256])
-        acc3b = accp.tile([P, 256], F32, name="acc3b", tag="acc")
-        mx_chunk(acc3b, LAST, 512, 256)
-        finish(v_copy, acc3b, 1792, 256, out_sb[LAST][:, 256:512])
+        for g in range(G):
+            vt_last(g)
+            q_w(LAST, 512 * g, 512)
+        acc3 = [
+            accp.tile([P, 256], F32, name="acc3%d" % h, tag="acc") for h in range(2)
+        ]
+        for g in range(G):
+            for h in range(2):
+                mx_part(acc3[h], LAST, 512 * g + 256 * h, 256, g)
+        last_view = out_sb[LAST][:].rearrange("j (m b) -> j m b", b=32)
+        for h in range(2):
+            (s_copy if h == 0 else v_copy)(
+                out=last_view[:, :, 16 * h : 16 * (h + 1)],
+                in_=acc3[h][:].rearrange("j (b m) -> j m b", m=16),
+            )
+        nc.sync.dma_start(out=out[:, 512 * LAST : O], in_=out_sb[LAST][:])

@@ -16,6 +16,7 @@ O = 2048
 G = K // 512
 NCH = 4
 T = 4
+NPE = 2
 LAST = NCH - 1
 
 FLOPS = 2 * R * P * K * O
@@ -55,46 +56,42 @@ def tile_testmmrsmodel_kernel(tc, hidden_states, gate_proj, world_size, out):
 
         half = T * K // 2
 
-        def load_w_halves(n):
-            view = gate_proj[512 * n : 512 * (n + 1), :].rearrange(
+        def w_rows(n):
+            return gate_proj[512 * n : 512 * (n + 1), :].rearrange(
                 "(p t) k -> p (t k)", t=T
             )
-            nc.sync.dma_start(out=w_raw[n][:, 0:half], in_=view[:, 0:half])
-            nc.sync.dma_start(out=w_raw[n][:, half:], in_=view[:, half:])
 
-        load_w_halves(0)
-        for r in range(R):
-            nc.sync.dma_start(out=x_raw[:, r * K : (r + 1) * K], in_=hidden_states[r])
-        nc.sync.dma_start(
-            out=w_raw[1][:],
-            in_=gate_proj[512:1024, :].rearrange("(p t) k -> p (t k)", t=T),
-        )
-        load_w_halves(2)
-        for g in range(G):
+        def load_pieces(n, g, b0, nb):
             for a in range(4):
                 for u in range(2):
                     k0 = 512 * g + 256 * u + 64 * a
                     nc.sync.dma_start(
-                        out=w_raw[LAST][
-                            32 * a + u : 32 * (a + 1) : 2, half * g : half * (g + 1)
+                        out=w_raw[n][
+                            32 * a + u : 32 * (a + 1) : 2,
+                            half * g + 64 * b0 : half * g + 64 * (b0 + nb),
                         ].rearrange("m (b k) -> m b k", k=64),
-                        in_=gate_proj[512 * LAST : O, k0 : k0 + 64].rearrange(
-                            "(m b) k -> m b k", b=32
-                        ),
+                        in_=gate_proj[
+                            512 * n : 512 * (n + 1), k0 : k0 + 64
+                        ].rearrange("(m b) k -> m b k", b=32)[:, b0 : b0 + nb, :],
                     )
+
+        nc.sync.dma_start(out=w_raw[0][:, 0:half], in_=w_rows(0)[:, 0:half])
+        nc.sync.dma_start(out=w_raw[0][:, half:], in_=w_rows(0)[:, half:])
+        for r in range(R):
+            nc.sync.dma_start(out=x_raw[:, r * K : (r + 1) * K], in_=hidden_states[r])
+        nc.sync.dma_start(out=w_raw[1][:], in_=w_rows(1))
+        load_pieces(2, 0, 0, 32)
+        load_pieces(2, 1, 0, 32)
+        load_pieces(LAST, 0, 0, 32)
+        load_pieces(LAST, 1, 0, 16)
+        load_pieces(LAST, 1, 16, 16)
 
         make_identity(nc, ident[:])
 
         x_words = x_raw[:].bitcast(F32)
         x_grp32 = x_grp[:].bitcast(F32)
         w_words = [w_raw[n][:].bitcast(F32) for n in range(NCH)]
-        w_grp32 = [
-            w_grp[n][:].bitcast(F32).rearrange(
-                "q (g t r u) -> q g t r u", g=G, t=T, u=2
-            )
-            for n in range(LAST)
-        ]
-        w_grp32_last = w_grp[LAST][:].bitcast(F32)
+        w_grp32 = [w_grp[n][:].bitcast(F32) for n in range(NCH)]
 
         def transpose_unit(words):
             bank = tp.tile([P, 4, P], F32, name="bank", tag="bank")
@@ -120,14 +117,16 @@ def tile_testmmrsmodel_kernel(tc, hidden_states, gate_proj, world_size, out):
 
         def c_w(copy, bank, n, t):
             copy(
-                out=w_grp32[n][:, :, t, :, :],
+                out=w_grp32[n].rearrange("q (g t r u) -> q g t r u", g=G, t=T, u=2)[
+                    :, :, t, :, :
+                ],
                 in_=bank[:].rearrange("q (g u) r -> q g r u", u=2),
             )
 
-        def vt_last(g):
+        def vt_w(n, first, count):
             nc.vector.transpose(
-                out=w_grp32_last[:, 1024 * g : 1024 * (g + 1)],
-                in_=w_words[LAST][:, 1024 * g : 1024 * (g + 1)],
+                out=w_grp32[n][:, first : first + count],
+                in_=w_words[n][:, first : first + count],
             )
 
         def q_x(r):
@@ -144,7 +143,7 @@ def tile_testmmrsmodel_kernel(tc, hidden_states, gate_proj, world_size, out):
                 in_=w_grp[n][:, 4 * first : 4 * (first + count)],
             )
 
-        def mx(acc, n, first, count, r, g, start, stop):
+        def mx(acc, n, first, count, r, g):
             xs = slice(256 * r + 128 * g, 256 * r + 128 * (g + 1))
             ws = slice(first, first + count)
             nc.tensor.matmul_mx(
@@ -153,20 +152,34 @@ def tile_testmmrsmodel_kernel(tc, hidden_states, gate_proj, world_size, out):
                 lhsT_scale=x_scales[:, xs],
                 rhs=w_codes[n][:, ws].bitcast(FP8X4),
                 rhs_scale=w_scales[n][:, ws],
-                start=start,
-                stop=stop,
+                start=(r == 0 and g == 0),
+                stop=(r == R - 1 and g == G - 1),
             )
 
-        def finish(copy, acc, first_col, count, dst):
-            rows = count // P
-            copy(
-                out=dst.rearrange("j (p t) -> j p t", t=rows),
-                in_=acc[:].rearrange("j (t p) -> j p t", t=rows),
-            )
-            nc.sync.dma_start(out=out[:, first_col : first_col + count], in_=dst)
+        def mx_part(acc, n, first, count, g):
+            for r in range(R):
+                mx(acc, n, first, count, r, g)
+
+        def store(n):
+            nc.sync.dma_start(out=out[:, 512 * n : 512 * (n + 1)], in_=out_sb[n][:])
 
         s_copy = nc.scalar.copy
         v_copy = nc.vector.tensor_copy
+
+        def finish_pe(copy, acc, n):
+            copy(
+                out=out_sb[n][:].rearrange("j (p t) -> j p t", t=T),
+                in_=acc[:].rearrange("j (t p) -> j p t", t=T),
+            )
+            store(n)
+
+        def copy_pieces(copy, acc, n, b0, nb):
+            copy(
+                out=out_sb[n][:].rearrange("j (m b) -> j m b", b=32)[
+                    :, :, b0 : b0 + nb
+                ],
+                in_=acc[:].rearrange("j (b m) -> j m b", m=16),
+            )
 
         b0 = t_w(0, 0)
         b1 = t_w(0, 1)
@@ -200,10 +213,7 @@ def tile_testmmrsmodel_kernel(tc, hidden_states, gate_proj, world_size, out):
         def mx_rows(rows):
             for r in rows:
                 for g in range(G):
-                    mx(
-                        acc0, 0, 512 * g, 512, r, g,
-                        r == 0 and g == 0, r == R - 1 and g == G - 1,
-                    )
+                    mx(acc0, 0, 512 * g, 512, r, g)
 
         mx_rows((0, 1))
         q_x(2)
@@ -220,55 +230,41 @@ def tile_testmmrsmodel_kernel(tc, hidden_states, gate_proj, world_size, out):
         mx_rows((2, 3, 4, 5))
 
         bw1 = [t_w(1, t) for t in range(T)]
-        bw2 = [t_w(2, t) for t in range(2)]
         c_w(v_copy, bw1[0], 1, 0)
         c_w(s_copy, bw1[1], 1, 1)
         c_w(v_copy, bw1[2], 1, 2)
         c_w(s_copy, bw1[3], 1, 3)
-        q_w(1, 0, 512)
+        q_w(1, 0, 256)
+        q_w(1, 256, 256)
         q_w(1, 512, 512)
-        c_w(s_copy, bw2[1], 2, 1)
-        c_w(v_copy, bw2[0], 2, 0)
         mx_rows((6, 7))
-        finish(s_copy, acc0, 0, 512, out_sb[0][:])
-        q_w(2, 0, 256)
-        q_w(2, 512, 256)
-
-        def mx_part(acc, n, first, count, g):
-            for r in range(R):
-                mx(
-                    acc, n, first, count, r, g,
-                    g == 0 and r == 0, g == G - 1 and r == R - 1,
-                )
+        finish_pe(s_copy, acc0, 0)
 
         acc1 = accp.tile([P, 512], F32, name="acc1", tag="acc")
         mx_part(acc1, 1, 0, 512, 0)
-        bw2 = [t_w(2, t) for t in range(2, T)]
-        c_w(v_copy, bw2[0], 2, 2)
-        c_w(s_copy, bw2[1], 2, 3)
-        q_w(2, 256, 256)
-        q_w(2, 768, 256)
         mx_part(acc1, 1, 512, 512, 1)
-        finish(s_copy, acc1, 512, 512, out_sb[1][:])
+        finish_pe(s_copy, acc1, 1)
 
+        for g in range(G):
+            vt_w(2, 1024 * g, 1024)
+            q_w(2, 512 * g, 512)
         acc2 = accp.tile([P, 512], F32, name="acc2", tag="acc")
         mx_part(acc2, 2, 0, 512, 0)
         mx_part(acc2, 2, 512, 512, 1)
-        finish(s_copy, acc2, 1024, 512, out_sb[2][:])
+        copy_pieces(s_copy, acc2, 2, 0, 32)
+        store(2)
 
-        for g in range(G):
-            vt_last(g)
-            q_w(LAST, 512 * g, 512)
+        vt_w(LAST, 0, 1024)
+        q_w(LAST, 0, 512)
+        for h in range(2):
+            vt_w(LAST, 1024 + 512 * h, 512)
+            q_w(LAST, 512 + 256 * h, 256)
         acc3 = [
             accp.tile([P, 256], F32, name="acc3%d" % h, tag="acc") for h in range(2)
         ]
         for g in range(G):
             for h in range(2):
                 mx_part(acc3[h], LAST, 512 * g + 256 * h, 256, g)
-        last_view = out_sb[LAST][:].rearrange("j (m b) -> j m b", b=32)
-        for h in range(2):
-            (s_copy if h == 0 else v_copy)(
-                out=last_view[:, :, 16 * h : 16 * (h + 1)],
-                in_=acc3[h][:].rearrange("j (b m) -> j m b", m=16),
-            )
-        nc.sync.dma_start(out=out[:, 512 * LAST : O], in_=out_sb[LAST][:])
+        copy_pieces(s_copy, acc3[0], LAST, 0, 16)
+        copy_pieces(v_copy, acc3[1], LAST, 16, 16)
+        store(LAST)

@@ -16,8 +16,8 @@ O = 2048
 G = K // 512
 NCH = 4
 T = 4
-NPE = 2
 LAST = NCH - 1
+PAD = 48
 
 FLOPS = 2 * R * P * K * O
 
@@ -34,8 +34,8 @@ def tile_testmmrsmodel_kernel(tc, hidden_states, gate_proj, world_size, out):
         ident = keep.tile([P, P], F32, name="ident")
         x_raw = keep.tile([P, R * K], BF16, name="x_raw")
         x_grp = keep.tile([P, R * K], BF16, name="x_grp", align_bytes=64)
-        x_codes = keep.tile([P, R * K // 4], U32, name="x_codes", align_bytes=64)
-        x_scales = keep.tile([P, R * K // 4], U8, name="x_scales", align_bytes=64)
+        x_codes = keep.tile([P, PAD + R * K // 4], U32, name="x_codes", align_bytes=256)
+        x_scales = keep.tile([P, R * G * 256], U8, name="x_scales", align_bytes=256)
         w_raw = [
             keep.tile([P, T * K], BF16, name="w_raw%d" % n, align_bytes=64)
             for n in range(NCH)
@@ -45,53 +45,57 @@ def tile_testmmrsmodel_kernel(tc, hidden_states, gate_proj, world_size, out):
             for n in range(NCH)
         ]
         w_codes = [
-            keep.tile([P, T * K // 4], U32, name="w_codes%d" % n, align_bytes=64)
+            keep.tile([P, T * K // 4], U32, name="w_codes%d" % n, align_bytes=256)
             for n in range(NCH)
         ]
         w_scales = [
-            keep.tile([P, T * K // 4], U8, name="w_scales%d" % n, align_bytes=64)
+            keep.tile([P, T * K // 4], U8, name="w_scales%d" % n, align_bytes=256)
             for n in range(NCH)
         ]
         out_sb = [keep.tile([P, 512], F32, name="out_sb%d" % n) for n in range(NCH)]
 
         half = T * K // 2
 
-        def w_rows(n):
-            return gate_proj[512 * n : 512 * (n + 1), :].rearrange(
+        def load_w_halves(n):
+            view = gate_proj[512 * n : 512 * (n + 1), :].rearrange(
                 "(p t) k -> p (t k)", t=T
             )
+            nc.sync.dma_start(out=w_raw[n][:, 0:half], in_=view[:, 0:half])
+            nc.sync.dma_start(out=w_raw[n][:, half:], in_=view[:, half:])
 
-        def load_pieces(n, g, b0, nb):
+        load_w_halves(0)
+        for r in range(R):
+            nc.sync.dma_start(out=x_raw[:, r * K : (r + 1) * K], in_=hidden_states[r])
+        nc.sync.dma_start(
+            out=w_raw[1][:],
+            in_=gate_proj[512:1024, :].rearrange("(p t) k -> p (t k)", t=T),
+        )
+        load_w_halves(2)
+        for g in range(G):
             for a in range(4):
                 for u in range(2):
                     k0 = 512 * g + 256 * u + 64 * a
                     nc.sync.dma_start(
-                        out=w_raw[n][
-                            32 * a + u : 32 * (a + 1) : 2,
-                            half * g + 64 * b0 : half * g + 64 * (b0 + nb),
+                        out=w_raw[LAST][
+                            32 * a + u : 32 * (a + 1) : 2, half * g : half * (g + 1)
                         ].rearrange("m (b k) -> m b k", k=64),
-                        in_=gate_proj[
-                            512 * n : 512 * (n + 1), k0 : k0 + 64
-                        ].rearrange("(m b) k -> m b k", b=32)[:, b0 : b0 + nb, :],
+                        in_=gate_proj[512 * LAST : O, k0 : k0 + 64].rearrange(
+                            "(m b) k -> m b k", b=32
+                        ),
                     )
-
-        nc.sync.dma_start(out=w_raw[0][:, 0:half], in_=w_rows(0)[:, 0:half])
-        nc.sync.dma_start(out=w_raw[0][:, half:], in_=w_rows(0)[:, half:])
-        for r in range(R):
-            nc.sync.dma_start(out=x_raw[:, r * K : (r + 1) * K], in_=hidden_states[r])
-        nc.sync.dma_start(out=w_raw[1][:], in_=w_rows(1))
-        load_pieces(2, 0, 0, 32)
-        load_pieces(2, 1, 0, 32)
-        load_pieces(LAST, 0, 0, 32)
-        load_pieces(LAST, 1, 0, 16)
-        load_pieces(LAST, 1, 16, 16)
 
         make_identity(nc, ident[:])
 
         x_words = x_raw[:].bitcast(F32)
         x_grp32 = x_grp[:].bitcast(F32)
         w_words = [w_raw[n][:].bitcast(F32) for n in range(NCH)]
-        w_grp32 = [w_grp[n][:].bitcast(F32) for n in range(NCH)]
+        w_grp32 = [
+            w_grp[n][:].bitcast(F32).rearrange(
+                "q (g t r u) -> q g t r u", g=G, t=T, u=2
+            )
+            for n in range(LAST)
+        ]
+        w_grp32_last = w_grp[LAST][:].bitcast(F32)
 
         def transpose_unit(words):
             bank = tp.tile([P, 4, P], F32, name="bank", tag="bank")
@@ -117,24 +121,24 @@ def tile_testmmrsmodel_kernel(tc, hidden_states, gate_proj, world_size, out):
 
         def c_w(copy, bank, n, t):
             copy(
-                out=w_grp32[n].rearrange("q (g t r u) -> q g t r u", g=G, t=T, u=2)[
-                    :, :, t, :, :
-                ],
+                out=w_grp32[n][:, :, t, :, :],
                 in_=bank[:].rearrange("q (g u) r -> q g r u", u=2),
             )
 
-        def vt_w(n, first, count):
+        def vt_last(g):
             nc.vector.transpose(
-                out=w_grp32[n][:, first : first + count],
-                in_=w_words[n][:, first : first + count],
+                out=w_grp32_last[:, 1024 * g : 1024 * (g + 1)],
+                in_=w_words[LAST][:, 1024 * g : 1024 * (g + 1)],
             )
 
         def q_x(r):
-            nc.vector.quantize_mx(
-                out=x_codes[:, 256 * r : 256 * (r + 1)].bitcast(FP8X4),
-                scales=x_scales[:, 256 * r : 256 * (r + 1)],
-                in_=x_grp[:, 1024 * r : 1024 * (r + 1)],
-            )
+            for g in range(G):
+                i = G * r + g
+                nc.vector.quantize_mx(
+                    out=x_codes[:, PAD + 128 * i : PAD + 128 * (i + 1)].bitcast(FP8X4),
+                    scales=x_scales[:, 256 * i : 256 * i + 128],
+                    in_=x_grp[:, 512 * i : 512 * (i + 1)],
+                )
 
         def q_w(n, first, count):
             nc.vector.quantize_mx(
@@ -143,43 +147,29 @@ def tile_testmmrsmodel_kernel(tc, hidden_states, gate_proj, world_size, out):
                 in_=w_grp[n][:, 4 * first : 4 * (first + count)],
             )
 
-        def mx(acc, n, first, count, r, g):
-            xs = slice(256 * r + 128 * g, 256 * r + 128 * (g + 1))
+        def mx(acc, n, first, count, r, g, start, stop):
+            i = G * r + g
             ws = slice(first, first + count)
             nc.tensor.matmul_mx(
                 out=acc[:],
-                lhsT=x_codes[:, xs].bitcast(FP8X4),
-                lhsT_scale=x_scales[:, xs],
+                lhsT=x_codes[:, PAD + 128 * i : PAD + 128 * (i + 1)].bitcast(FP8X4),
+                lhsT_scale=x_scales[:, 256 * i : 256 * i + 128],
                 rhs=w_codes[n][:, ws].bitcast(FP8X4),
                 rhs_scale=w_scales[n][:, ws],
-                start=(r == 0 and g == 0),
-                stop=(r == R - 1 and g == G - 1),
+                start=start,
+                stop=stop,
             )
 
-        def mx_part(acc, n, first, count, g):
-            for r in range(R):
-                mx(acc, n, first, count, r, g)
-
-        def store(n):
-            nc.sync.dma_start(out=out[:, 512 * n : 512 * (n + 1)], in_=out_sb[n][:])
+        def finish(copy, acc, first_col, count, dst):
+            rows = count // P
+            copy(
+                out=dst.rearrange("j (p t) -> j p t", t=rows),
+                in_=acc[:].rearrange("j (t p) -> j p t", t=rows),
+            )
+            nc.sync.dma_start(out=out[:, first_col : first_col + count], in_=dst)
 
         s_copy = nc.scalar.copy
         v_copy = nc.vector.tensor_copy
-
-        def finish_pe(copy, acc, n):
-            copy(
-                out=out_sb[n][:].rearrange("j (p t) -> j p t", t=T),
-                in_=acc[:].rearrange("j (t p) -> j p t", t=T),
-            )
-            store(n)
-
-        def copy_pieces(copy, acc, n, b0, nb):
-            copy(
-                out=out_sb[n][:].rearrange("j (m b) -> j m b", b=32)[
-                    :, :, b0 : b0 + nb
-                ],
-                in_=acc[:].rearrange("j (b m) -> j m b", m=16),
-            )
 
         b0 = t_w(0, 0)
         b1 = t_w(0, 1)
@@ -213,7 +203,10 @@ def tile_testmmrsmodel_kernel(tc, hidden_states, gate_proj, world_size, out):
         def mx_rows(rows):
             for r in rows:
                 for g in range(G):
-                    mx(acc0, 0, 512 * g, 512, r, g)
+                    mx(
+                        acc0, 0, 512 * g, 512, r, g,
+                        r == 0 and g == 0, r == R - 1 and g == G - 1,
+                    )
 
         mx_rows((0, 1))
         q_x(2)
@@ -230,41 +223,55 @@ def tile_testmmrsmodel_kernel(tc, hidden_states, gate_proj, world_size, out):
         mx_rows((2, 3, 4, 5))
 
         bw1 = [t_w(1, t) for t in range(T)]
+        bw2 = [t_w(2, t) for t in range(2)]
         c_w(v_copy, bw1[0], 1, 0)
         c_w(s_copy, bw1[1], 1, 1)
         c_w(v_copy, bw1[2], 1, 2)
         c_w(s_copy, bw1[3], 1, 3)
-        q_w(1, 0, 256)
-        q_w(1, 256, 256)
+        q_w(1, 0, 512)
         q_w(1, 512, 512)
+        c_w(s_copy, bw2[1], 2, 1)
+        c_w(v_copy, bw2[0], 2, 0)
         mx_rows((6, 7))
-        finish_pe(s_copy, acc0, 0)
+        finish(s_copy, acc0, 0, 512, out_sb[0][:])
+        q_w(2, 0, 256)
+        q_w(2, 512, 256)
+
+        def mx_part(acc, n, first, count, g):
+            for r in range(R):
+                mx(
+                    acc, n, first, count, r, g,
+                    g == 0 and r == 0, g == G - 1 and r == R - 1,
+                )
 
         acc1 = accp.tile([P, 512], F32, name="acc1", tag="acc")
         mx_part(acc1, 1, 0, 512, 0)
+        bw2 = [t_w(2, t) for t in range(2, T)]
+        c_w(v_copy, bw2[0], 2, 2)
+        c_w(s_copy, bw2[1], 2, 3)
+        q_w(2, 256, 256)
+        q_w(2, 768, 256)
         mx_part(acc1, 1, 512, 512, 1)
-        finish_pe(s_copy, acc1, 1)
+        finish(s_copy, acc1, 512, 512, out_sb[1][:])
 
-        for g in range(G):
-            vt_w(2, 1024 * g, 1024)
-            q_w(2, 512 * g, 512)
         acc2 = accp.tile([P, 512], F32, name="acc2", tag="acc")
         mx_part(acc2, 2, 0, 512, 0)
         mx_part(acc2, 2, 512, 512, 1)
-        copy_pieces(s_copy, acc2, 2, 0, 32)
-        store(2)
+        finish(s_copy, acc2, 1024, 512, out_sb[2][:])
 
-        vt_w(LAST, 0, 1024)
-        q_w(LAST, 0, 512)
-        for h in range(2):
-            vt_w(LAST, 1024 + 512 * h, 512)
-            q_w(LAST, 512 + 256 * h, 256)
+        for g in range(G):
+            vt_last(g)
+            q_w(LAST, 512 * g, 512)
         acc3 = [
             accp.tile([P, 256], F32, name="acc3%d" % h, tag="acc") for h in range(2)
         ]
         for g in range(G):
             for h in range(2):
                 mx_part(acc3[h], LAST, 512 * g + 256 * h, 256, g)
-        copy_pieces(s_copy, acc3[0], LAST, 0, 16)
-        copy_pieces(v_copy, acc3[1], LAST, 16, 16)
-        store(LAST)
+        last_view = out_sb[LAST][:].rearrange("j (m b) -> j m b", b=32)
+        for h in range(2):
+            (s_copy if h == 0 else v_copy)(
+                out=last_view[:, :, 16 * h : 16 * (h + 1)],
+                in_=acc3[h][:].rearrange("j (b m) -> j m b", m=16),
+            )
+        nc.sync.dma_start(out=out[:, 512 * LAST : O], in_=out_sb[LAST][:])

@@ -14,10 +14,16 @@ R = 8
 K = 1024
 O = 2048
 G = K // 512
-NCH = 4
-T = 4
-LAST = NCH - 1
-PAD = 48
+WORDS = K // 2
+CHUNK = 512
+CHUNKS = O // CHUNK
+TILES = CHUNK // P
+LAST = CHUNKS - 1
+BLOCK = 32
+ROWS_M = BLOCK // 2
+HALF = CHUNK // 2
+TRANSPOSE_BANKS = 6
+SUM_BANKS = 2
 
 FLOPS = 2 * R * P * K * O
 
@@ -27,251 +33,219 @@ def tile_testmmrsmodel_kernel(tc, hidden_states, gate_proj, world_size, out):
     assert world_size == R
     with ExitStack() as ctx:
         keep = ctx.enter_context(tc.tile_pool(name="keep", bufs=1))
-        tp = ctx.enter_context(tc.psum_pool(name="tp", bufs=6))
-        accp = ctx.enter_context(tc.psum_pool(name="accp", bufs=2))
+        transposed = ctx.enter_context(tc.psum_pool(name="transposed", bufs=TRANSPOSE_BANKS))
+        sums = ctx.enter_context(tc.psum_pool(name="sums", bufs=SUM_BANKS))
         ctx.enter_context(tc.manual_schedule())
 
         ident = keep.tile([P, P], F32, name="ident")
         x_raw = keep.tile([P, R * K], BF16, name="x_raw")
-        x_grp = keep.tile([P, R * K], BF16, name="x_grp", align_bytes=64)
-        x_codes = keep.tile([P, PAD + R * K // 4], U32, name="x_codes", align_bytes=256)
-        x_scales = keep.tile([P, R * G * 256], U8, name="x_scales", align_bytes=256)
+        x_grouped = keep.tile([P, R * K], BF16, name="x_grouped", align_bytes=64)
+        x_codes = keep.tile([P, R * K // 4], U32, name="x_codes", align_bytes=64)
+        x_scales = keep.tile([P, R * K // 4], U8, name="x_scales", align_bytes=64)
         w_raw = [
-            keep.tile([P, T * K], BF16, name="w_raw%d" % n, align_bytes=64)
-            for n in range(NCH)
+            keep.tile([P, TILES * K], BF16, name="w_raw%d" % n, align_bytes=64)
+            for n in range(CHUNKS)
         ]
-        w_grp = [
-            keep.tile([P, T * K], BF16, name="w_grp%d" % n, align_bytes=64)
-            for n in range(NCH)
+        w_grouped = [
+            keep.tile([P, TILES * K], BF16, name="w_grouped%d" % n, align_bytes=64)
+            for n in range(CHUNKS)
         ]
         w_codes = [
-            keep.tile([P, T * K // 4], U32, name="w_codes%d" % n, align_bytes=256)
-            for n in range(NCH)
+            keep.tile([P, G * CHUNK], U32, name="w_codes%d" % n, align_bytes=64)
+            for n in range(CHUNKS)
         ]
         w_scales = [
-            keep.tile([P, T * K // 4], U8, name="w_scales%d" % n, align_bytes=256)
-            for n in range(NCH)
+            keep.tile([P, G * CHUNK], U8, name="w_scales%d" % n, align_bytes=64)
+            for n in range(CHUNKS)
         ]
-        out_sb = [keep.tile([P, 512], F32, name="out_sb%d" % n) for n in range(NCH)]
+        out_sb = [keep.tile([P, CHUNK], F32, name="out_sb%d" % n) for n in range(CHUNKS)]
 
-        half = T * K // 2
-
-        def load_w_halves(n):
-            view = gate_proj[512 * n : 512 * (n + 1), :].rearrange(
-                "(p t) k -> p (t k)", t=T
+        def load_tiles(n, first_tile, tiles):
+            rows = gate_proj[CHUNK * n : CHUNK * (n + 1), :].rearrange(
+                "(p t) k -> p (t k)", t=TILES
             )
-            nc.sync.dma_start(out=w_raw[n][:, 0:half], in_=view[:, 0:half])
-            nc.sync.dma_start(out=w_raw[n][:, half:], in_=view[:, half:])
+            cols = slice(first_tile * K, (first_tile + tiles) * K)
+            nc.sync.dma_start(out=w_raw[n][:, cols], in_=rows[:, cols])
 
-        load_w_halves(0)
+        load_tiles(0, 0, 2)
+        load_tiles(0, 2, 2)
         for r in range(R):
             nc.sync.dma_start(out=x_raw[:, r * K : (r + 1) * K], in_=hidden_states[r])
-        nc.sync.dma_start(
-            out=w_raw[1][:],
-            in_=gate_proj[512:1024, :].rearrange("(p t) k -> p (t k)", t=T),
-        )
-        load_w_halves(2)
+        load_tiles(1, 0, TILES)
+        load_tiles(2, 0, 2)
+        load_tiles(2, 2, 2)
+        last_rows = gate_proj[CHUNK * LAST : O, :].rearrange("(m b) k -> m b k", b=BLOCK)
         for g in range(G):
-            for a in range(4):
+            for a in range(P // BLOCK):
                 for u in range(2):
-                    k0 = 512 * g + 256 * u + 64 * a
+                    k0 = 512 * g + 256 * u + 2 * BLOCK * a
                     nc.sync.dma_start(
                         out=w_raw[LAST][
-                            32 * a + u : 32 * (a + 1) : 2, half * g : half * (g + 1)
-                        ].rearrange("m (b k) -> m b k", k=64),
-                        in_=gate_proj[512 * LAST : O, k0 : k0 + 64].rearrange(
-                            "(m b) k -> m b k", b=32
-                        ),
+                            BLOCK * a + u : BLOCK * (a + 1) : 2,
+                            2 * K * g : 2 * K * (g + 1),
+                        ].rearrange("m (b k) -> m b k", k=2 * BLOCK),
+                        in_=last_rows[:, :, k0 : k0 + 2 * BLOCK],
                     )
 
         make_identity(nc, ident[:])
 
         x_words = x_raw[:].bitcast(F32)
-        x_grp32 = x_grp[:].bitcast(F32)
-        w_words = [w_raw[n][:].bitcast(F32) for n in range(NCH)]
-        w_grp32 = [
-            w_grp[n][:].bitcast(F32).rearrange(
-                "q (g t r u) -> q g t r u", g=G, t=T, u=2
-            )
-            for n in range(LAST)
-        ]
-        w_grp32_last = w_grp[LAST][:].bitcast(F32)
+        x_grouped_words = x_grouped[:].bitcast(F32)
+        w_words = [w_raw[n][:].bitcast(F32) for n in range(CHUNKS)]
+        w_grouped_words = [w_grouped[n][:].bitcast(F32) for n in range(CHUNKS)]
 
-        def transpose_unit(words):
-            bank = tp.tile([P, 4, P], F32, name="bank", tag="bank")
-            for c in range(4):
-                nc.tensor.transpose(
-                    bank[:, c, :], words[:, c * P : (c + 1) * P], ident[:]
-                )
+        scalar_copy = nc.scalar.copy
+        vector_copy = nc.vector.tensor_copy
+
+        def transpose_tile(words):
+            bank = transposed.tile([P, WORDS // P, P], F32, name="bank", tag="bank")
+            for c in range(WORDS // P):
+                nc.tensor.transpose(bank[:, c, :], words[:, c * P : (c + 1) * P], ident[:])
             return bank
 
-        def t_x(r):
-            return transpose_unit(x_words[:, 512 * r : 512 * (r + 1)])
+        def transpose_x(r):
+            return transpose_tile(x_words[:, WORDS * r : WORDS * (r + 1)])
 
-        def t_w(n, t):
-            return transpose_unit(w_words[n][:, 512 * t : 512 * (t + 1)])
+        def transpose_w(n, t):
+            return transpose_tile(w_words[n][:, WORDS * t : WORDS * (t + 1)])
 
-        def c_x(copy, bank, r):
-            copy(
-                out=x_grp32[:, 512 * r : 512 * (r + 1)].rearrange(
-                    "q (g r u) -> q g r u", g=G, u=2
+        def regroup(copy, bank, grouped_view):
+            copy(out=grouped_view, in_=bank[:].rearrange("p (g u) row -> p g row u", u=2))
+
+        def regroup_x(bank, r):
+            regroup(
+                scalar_copy,
+                bank,
+                x_grouped_words[:, WORDS * r : WORDS * (r + 1)].rearrange(
+                    "p (g row u) -> p g row u", g=G, u=2
                 ),
-                in_=bank[:].rearrange("q (g u) r -> q g r u", u=2),
             )
 
-        def c_w(copy, bank, n, t):
-            copy(
-                out=w_grp32[n][:, :, t, :, :],
-                in_=bank[:].rearrange("q (g u) r -> q g r u", u=2),
+        def regroup_w(bank, n, t):
+            regroup(
+                vector_copy if t % 2 == 0 else scalar_copy,
+                bank,
+                w_grouped_words[n].rearrange(
+                    "p (g t row u) -> p g t row u", g=G, t=TILES, u=2
+                )[:, :, t, :, :],
             )
 
-        def vt_last(g):
-            nc.vector.transpose(
-                out=w_grp32_last[:, 1024 * g : 1024 * (g + 1)],
-                in_=w_words[LAST][:, 1024 * g : 1024 * (g + 1)],
-            )
-
-        def q_x(r):
-            for g in range(G):
-                i = G * r + g
+        def quantise_x(r):
+            for i in range(G * r, G * (r + 1)):
                 nc.vector.quantize_mx(
-                    out=x_codes[:, PAD + 128 * i : PAD + 128 * (i + 1)].bitcast(FP8X4),
-                    scales=x_scales[:, 256 * i : 256 * i + 128],
-                    in_=x_grp[:, 512 * i : 512 * (i + 1)],
+                    out=x_codes[:, P * i : P * (i + 1)].bitcast(FP8X4),
+                    scales=x_scales[:, P * i : P * (i + 1)],
+                    in_=x_grouped[:, 4 * P * i : 4 * P * (i + 1)],
                 )
 
-        def q_w(n, first, count):
+        def quantise_w(n, g, first, count):
+            lo = CHUNK * g + first
             nc.vector.quantize_mx(
-                out=w_codes[n][:, first : first + count].bitcast(FP8X4),
-                scales=w_scales[n][:, first : first + count],
-                in_=w_grp[n][:, 4 * first : 4 * (first + count)],
+                out=w_codes[n][:, lo : lo + count].bitcast(FP8X4),
+                scales=w_scales[n][:, lo : lo + count],
+                in_=w_grouped[n][:, 4 * lo : 4 * (lo + count)],
             )
 
-        def mx(acc, n, first, count, r, g, start, stop):
-            i = G * r + g
-            ws = slice(first, first + count)
-            nc.tensor.matmul_mx(
-                out=acc[:],
-                lhsT=x_codes[:, PAD + 128 * i : PAD + 128 * (i + 1)].bitcast(FP8X4),
-                lhsT_scale=x_scales[:, 256 * i : 256 * i + 128],
-                rhs=w_codes[n][:, ws].bitcast(FP8X4),
-                rhs_scale=w_scales[n][:, ws],
-                start=start,
-                stop=stop,
+        def passes(acc, n, g, first, count, rows):
+            cols = slice(CHUNK * g + first, CHUNK * g + first + count)
+            for r in rows:
+                i = G * r + g
+                nc.tensor.matmul_mx(
+                    out=acc[:],
+                    lhsT=x_codes[:, P * i : P * (i + 1)].bitcast(FP8X4),
+                    lhsT_scale=x_scales[:, P * i : P * (i + 1)],
+                    rhs=w_codes[n][:, cols].bitcast(FP8X4),
+                    rhs_scale=w_scales[n][:, cols],
+                    start=(r == 0 and g == 0),
+                    stop=(r == R - 1 and g == G - 1),
+                )
+
+        def store(n):
+            nc.sync.dma_start(out=out[:, CHUNK * n : CHUNK * (n + 1)], in_=out_sb[n][:])
+
+        def leave(acc, n):
+            scalar_copy(
+                out=out_sb[n][:].rearrange("j (p t) -> j p t", t=TILES),
+                in_=acc[:].rearrange("j (t p) -> j p t", t=TILES),
             )
+            store(n)
 
-        def finish(copy, acc, first_col, count, dst):
-            rows = count // P
-            copy(
-                out=dst.rearrange("j (p t) -> j p t", t=rows),
-                in_=acc[:].rearrange("j (t p) -> j p t", t=rows),
-            )
-            nc.sync.dma_start(out=out[:, first_col : first_col + count], in_=dst)
+        all_rows = range(R)
 
-        s_copy = nc.scalar.copy
-        v_copy = nc.vector.tensor_copy
+        for first_tile in (0, 2):
+            pair = (first_tile, first_tile + 1)
+            banks = [transpose_w(0, t) for t in pair]
+            for t in pair:
+                regroup_w(banks[t - first_tile], 0, t)
+            for t in reversed(pair):
+                for g in range(G):
+                    quantise_w(0, g, P * t, P)
 
-        b0 = t_w(0, 0)
-        b1 = t_w(0, 1)
-        c_w(s_copy, b0, 0, 0)
-        c_w(v_copy, b1, 0, 1)
-        b2 = t_w(0, 2)
-        b3 = t_w(0, 3)
-        q_w(0, 0, 128)
-        q_w(0, 512, 128)
-        c_w(s_copy, b2, 0, 2)
-        q_w(0, 128, 128)
-        q_w(0, 640, 128)
-        c_w(v_copy, b3, 0, 3)
-        bx = t_x(0)
-        c_x(s_copy, bx, 0)
-        q_w(0, 256, 128)
-        q_w(0, 768, 128)
-        bx = t_x(1)
-        c_x(s_copy, bx, 1)
-        q_w(0, 384, 128)
-        q_w(0, 896, 128)
-        q_x(0)
-        bx = t_x(2)
-        c_x(s_copy, bx, 2)
-        q_x(1)
-        bx = t_x(3)
-        c_x(s_copy, bx, 3)
+        def prepare_x(rows):
+            banks = [transpose_x(r) for r in rows]
+            for r in rows:
+                regroup_x(banks[r - rows[0]], r)
+                quantise_x(r)
 
-        acc0 = accp.tile([P, 512], F32, name="acc0", tag="acc")
-
-        def mx_rows(rows):
+        def passes_chunk0(acc, rows):
             for r in rows:
                 for g in range(G):
-                    mx(
-                        acc0, 0, 512 * g, 512, r, g,
-                        r == 0 and g == 0, r == R - 1 and g == G - 1,
-                    )
+                    passes(acc, 0, g, 0, CHUNK, (r,))
 
-        mx_rows((0, 1))
-        q_x(2)
-        q_x(3)
-        bxs = [t_x(r) for r in range(4, 8)]
-        c_x(s_copy, bxs[0], 4)
-        c_x(v_copy, bxs[1], 5)
-        q_x(4)
-        c_x(s_copy, bxs[2], 6)
-        c_x(v_copy, bxs[3], 7)
-        q_x(5)
-        q_x(6)
-        q_x(7)
-        mx_rows((2, 3, 4, 5))
+        acc0 = sums.tile([P, CHUNK], F32, name="acc0", tag="acc")
+        prepare_x((0, 1, 2, 3))
+        passes_chunk0(acc0, (0, 1))
+        prepare_x((4, 5, 6, 7))
+        passes_chunk0(acc0, (2, 3, 4, 5))
 
-        bw1 = [t_w(1, t) for t in range(T)]
-        bw2 = [t_w(2, t) for t in range(2)]
-        c_w(v_copy, bw1[0], 1, 0)
-        c_w(s_copy, bw1[1], 1, 1)
-        c_w(v_copy, bw1[2], 1, 2)
-        c_w(s_copy, bw1[3], 1, 3)
-        q_w(1, 0, 512)
-        q_w(1, 512, 512)
-        c_w(s_copy, bw2[1], 2, 1)
-        c_w(v_copy, bw2[0], 2, 0)
-        mx_rows((6, 7))
-        finish(s_copy, acc0, 0, 512, out_sb[0][:])
-        q_w(2, 0, 256)
-        q_w(2, 512, 256)
+        banks1 = [transpose_w(1, t) for t in range(TILES)]
+        banks2 = [transpose_w(2, t) for t in (0, 1)]
+        for t in range(TILES):
+            regroup_w(banks1[t], 1, t)
+        for g in range(G):
+            quantise_w(1, g, 0, CHUNK)
+        for t in (0, 1):
+            regroup_w(banks2[t], 2, t)
+        passes_chunk0(acc0, (6, 7))
+        leave(acc0, 0)
+        for g in range(G):
+            quantise_w(2, g, 0, HALF)
 
-        def mx_part(acc, n, first, count, g):
-            for r in range(R):
-                mx(
-                    acc, n, first, count, r, g,
-                    g == 0 and r == 0, g == G - 1 and r == R - 1,
-                )
+        acc1 = sums.tile([P, CHUNK], F32, name="acc1", tag="acc")
+        passes(acc1, 1, 0, 0, CHUNK, all_rows)
+        banks2 = [transpose_w(2, t) for t in (2, 3)]
+        for t in (2, 3):
+            regroup_w(banks2[t - 2], 2, t)
+        for g in range(G):
+            quantise_w(2, g, HALF, HALF)
+        passes(acc1, 1, 1, 0, CHUNK, all_rows)
+        leave(acc1, 1)
 
-        acc1 = accp.tile([P, 512], F32, name="acc1", tag="acc")
-        mx_part(acc1, 1, 0, 512, 0)
-        bw2 = [t_w(2, t) for t in range(2, T)]
-        c_w(v_copy, bw2[0], 2, 2)
-        c_w(s_copy, bw2[1], 2, 3)
-        q_w(2, 256, 256)
-        q_w(2, 768, 256)
-        mx_part(acc1, 1, 512, 512, 1)
-        finish(s_copy, acc1, 512, 512, out_sb[1][:])
-
-        acc2 = accp.tile([P, 512], F32, name="acc2", tag="acc")
-        mx_part(acc2, 2, 0, 512, 0)
-        mx_part(acc2, 2, 512, 512, 1)
-        finish(s_copy, acc2, 1024, 512, out_sb[2][:])
+        acc2 = sums.tile([P, CHUNK], F32, name="acc2", tag="acc")
+        for g in range(G):
+            passes(acc2, 2, g, 0, CHUNK, all_rows)
+        leave(acc2, 2)
 
         for g in range(G):
-            vt_last(g)
-            q_w(LAST, 512 * g, 512)
-        acc3 = [
-            accp.tile([P, 256], F32, name="acc3%d" % h, tag="acc") for h in range(2)
+            for h in range(2):
+                first_word = WORDS * 2 * g + WORDS * h
+                nc.vector.transpose(
+                    out=w_grouped_words[LAST][:, first_word : first_word + WORDS],
+                    in_=w_words[LAST][:, first_word : first_word + WORDS],
+                )
+                quantise_w(LAST, g, HALF * h, HALF)
+        acc_last = [
+            sums.tile([P, HALF], F32, name="acc_last%d" % h, tag="acc") for h in range(2)
         ]
         for g in range(G):
             for h in range(2):
-                mx_part(acc3[h], LAST, 512 * g + 256 * h, 256, g)
-        last_view = out_sb[LAST][:].rearrange("j (m b) -> j m b", b=32)
+                passes(acc_last[h], LAST, g, HALF * h, HALF, all_rows)
+        blocks_of_half = BLOCK // 2
         for h in range(2):
-            (s_copy if h == 0 else v_copy)(
-                out=last_view[:, :, 16 * h : 16 * (h + 1)],
-                in_=acc3[h][:].rearrange("j (b m) -> j m b", m=16),
+            (scalar_copy if h == 0 else vector_copy)(
+                out=out_sb[LAST][:].rearrange("j (m b) -> j m b", b=BLOCK)[
+                    :, :, blocks_of_half * h : blocks_of_half * (h + 1)
+                ],
+                in_=acc_last[h][:].rearrange("j (b m) -> j m b", m=ROWS_M),
             )
-        nc.sync.dma_start(out=out[:, 512 * LAST : O], in_=out_sb[LAST][:])
+        store(LAST)

from contextlib import ExitStack

import concourse.mybir as mybir
from concourse.masks import make_identity

F32 = mybir.dt.float32
BF16 = mybir.dt.bfloat16
U32 = mybir.dt.uint32
U8 = mybir.dt.uint8
FP8X4 = mybir.dt.float8_e4m3fn_x4

P = 128
R = 8
K = 1024
O = 2048
G = K // 512
WORDS = K // 2
CHUNK = 512
CHUNKS = O // CHUNK
TILES = CHUNK // P
LAST = CHUNKS - 1
BLOCK = 32
ROWS_M = BLOCK // 2
HALF = CHUNK // 2
TRANSPOSE_BANKS = 6
SUM_BANKS = 2

FLOPS = 2 * R * P * K * O


def tile_testmmrsmodel_kernel(tc, hidden_states, gate_proj, world_size, out):
    nc = tc.nc
    assert world_size == R
    with ExitStack() as ctx:
        keep = ctx.enter_context(tc.tile_pool(name="keep", bufs=1))
        transposed = ctx.enter_context(tc.psum_pool(name="transposed", bufs=TRANSPOSE_BANKS))
        sums = ctx.enter_context(tc.psum_pool(name="sums", bufs=SUM_BANKS))
        ctx.enter_context(tc.manual_schedule())

        ident = keep.tile([P, P], F32, name="ident")
        x_raw = keep.tile([P, R * K], BF16, name="x_raw")
        x_grouped = keep.tile([P, R * K], BF16, name="x_grouped", align_bytes=64)
        x_codes = keep.tile([P, R * K // 4], U32, name="x_codes", align_bytes=64)
        x_scales = keep.tile([P, R * K // 4], U8, name="x_scales", align_bytes=64)
        w_raw = [
            keep.tile([P, TILES * K], BF16, name="w_raw%d" % n, align_bytes=64)
            for n in range(CHUNKS)
        ]
        w_grouped = [
            keep.tile([P, TILES * K], BF16, name="w_grouped%d" % n, align_bytes=64)
            for n in range(CHUNKS)
        ]
        w_codes = [
            keep.tile([P, G * CHUNK], U32, name="w_codes%d" % n, align_bytes=64)
            for n in range(CHUNKS)
        ]
        w_scales = [
            keep.tile([P, G * CHUNK], U8, name="w_scales%d" % n, align_bytes=64)
            for n in range(CHUNKS)
        ]
        out_sb = [keep.tile([P, CHUNK], F32, name="out_sb%d" % n) for n in range(CHUNKS)]

        def load_tiles(n, first_tile, tiles):
            rows = gate_proj[CHUNK * n : CHUNK * (n + 1), :].rearrange(
                "(p t) k -> p (t k)", t=TILES
            )
            cols = slice(first_tile * K, (first_tile + tiles) * K)
            nc.sync.dma_start(out=w_raw[n][:, cols], in_=rows[:, cols])

        load_tiles(0, 0, 2)
        load_tiles(0, 2, 2)
        for r in range(R):
            nc.sync.dma_start(out=x_raw[:, r * K : (r + 1) * K], in_=hidden_states[r])
        load_tiles(1, 0, TILES)
        load_tiles(2, 0, 2)
        load_tiles(2, 2, 2)
        last_rows = gate_proj[CHUNK * LAST : O, :].rearrange("(m b) k -> m b k", b=BLOCK)
        for g in range(G):
            for a in range(P // BLOCK):
                for u in range(2):
                    k0 = 512 * g + 256 * u + 2 * BLOCK * a
                    nc.sync.dma_start(
                        out=w_raw[LAST][
                            BLOCK * a + u : BLOCK * (a + 1) : 2,
                            2 * K * g : 2 * K * (g + 1),
                        ].rearrange("m (b k) -> m b k", k=2 * BLOCK),
                        in_=last_rows[:, :, k0 : k0 + 2 * BLOCK],
                    )

        make_identity(nc, ident[:])

        x_words = x_raw[:].bitcast(F32)
        x_grouped_words = x_grouped[:].bitcast(F32)
        w_words = [w_raw[n][:].bitcast(F32) for n in range(CHUNKS)]
        w_grouped_words = [w_grouped[n][:].bitcast(F32) for n in range(CHUNKS)]

        scalar_copy = nc.scalar.copy
        vector_copy = nc.vector.tensor_copy

        def transpose_tile(words):
            bank = transposed.tile([P, WORDS // P, P], F32, name="bank", tag="bank")
            for c in range(WORDS // P):
                nc.tensor.transpose(bank[:, c, :], words[:, c * P : (c + 1) * P], ident[:])
            return bank

        def transpose_x(r):
            return transpose_tile(x_words[:, WORDS * r : WORDS * (r + 1)])

        def transpose_w(n, t):
            return transpose_tile(w_words[n][:, WORDS * t : WORDS * (t + 1)])

        def regroup(copy, bank, grouped_view):
            copy(out=grouped_view, in_=bank[:].rearrange("p (g u) row -> p g row u", u=2))

        def regroup_x(bank, r):
            regroup(
                scalar_copy,
                bank,
                x_grouped_words[:, WORDS * r : WORDS * (r + 1)].rearrange(
                    "p (g row u) -> p g row u", g=G, u=2
                ),
            )

        def regroup_w(bank, n, t):
            regroup(
                vector_copy if t % 2 == 0 else scalar_copy,
                bank,
                w_grouped_words[n].rearrange(
                    "p (g t row u) -> p g t row u", g=G, t=TILES, u=2
                )[:, :, t, :, :],
            )

        def quantise_x(r):
            for i in range(G * r, G * (r + 1)):
                nc.vector.quantize_mx(
                    out=x_codes[:, P * i : P * (i + 1)].bitcast(FP8X4),
                    scales=x_scales[:, P * i : P * (i + 1)],
                    in_=x_grouped[:, 4 * P * i : 4 * P * (i + 1)],
                )

        def quantise_w(n, g, first, count):
            lo = CHUNK * g + first
            nc.vector.quantize_mx(
                out=w_codes[n][:, lo : lo + count].bitcast(FP8X4),
                scales=w_scales[n][:, lo : lo + count],
                in_=w_grouped[n][:, 4 * lo : 4 * (lo + count)],
            )

        def passes(acc, n, g, first, count, rows):
            cols = slice(CHUNK * g + first, CHUNK * g + first + count)
            for r in rows:
                i = G * r + g
                nc.tensor.matmul_mx(
                    out=acc[:],
                    lhsT=x_codes[:, P * i : P * (i + 1)].bitcast(FP8X4),
                    lhsT_scale=x_scales[:, P * i : P * (i + 1)],
                    rhs=w_codes[n][:, cols].bitcast(FP8X4),
                    rhs_scale=w_scales[n][:, cols],
                    start=(r == 0 and g == 0),
                    stop=(r == R - 1 and g == G - 1),
                )

        def store(n):
            nc.sync.dma_start(out=out[:, CHUNK * n : CHUNK * (n + 1)], in_=out_sb[n][:])

        def leave(acc, n):
            scalar_copy(
                out=out_sb[n][:].rearrange("j (p t) -> j p t", t=TILES),
                in_=acc[:].rearrange("j (t p) -> j p t", t=TILES),
            )
            store(n)

        all_rows = range(R)

        for first_tile in (0, 2):
            pair = (first_tile, first_tile + 1)
            banks = [transpose_w(0, t) for t in pair]
            for t in pair:
                regroup_w(banks[t - first_tile], 0, t)
            for t in reversed(pair):
                for g in range(G):
                    quantise_w(0, g, P * t, P)

        def prepare_x(rows):
            banks = [transpose_x(r) for r in rows]
            for r in rows:
                regroup_x(banks[r - rows[0]], r)
                quantise_x(r)

        def passes_chunk0(acc, rows):
            for r in rows:
                for g in range(G):
                    passes(acc, 0, g, 0, CHUNK, (r,))

        acc0 = sums.tile([P, CHUNK], F32, name="acc0", tag="acc")
        prepare_x((0, 1, 2, 3))
        passes_chunk0(acc0, (0, 1))
        prepare_x((4, 5, 6, 7))
        passes_chunk0(acc0, (2, 3, 4, 5))

        banks1 = [transpose_w(1, t) for t in range(TILES)]
        banks2 = [transpose_w(2, t) for t in (0, 1)]
        for t in range(TILES):
            regroup_w(banks1[t], 1, t)
        for g in range(G):
            quantise_w(1, g, 0, CHUNK)
        for t in (0, 1):
            regroup_w(banks2[t], 2, t)
        passes_chunk0(acc0, (6, 7))
        leave(acc0, 0)
        for g in range(G):
            quantise_w(2, g, 0, HALF)

        acc1 = sums.tile([P, CHUNK], F32, name="acc1", tag="acc")
        passes(acc1, 1, 0, 0, CHUNK, all_rows)
        banks2 = [transpose_w(2, t) for t in (2, 3)]
        for t in (2, 3):
            regroup_w(banks2[t - 2], 2, t)
        for g in range(G):
            quantise_w(2, g, HALF, HALF)
        passes(acc1, 1, 1, 0, CHUNK, all_rows)
        leave(acc1, 1)

        acc2 = sums.tile([P, CHUNK], F32, name="acc2", tag="acc")
        for g in range(G):
            passes(acc2, 2, g, 0, CHUNK, all_rows)
        leave(acc2, 2)

        for g in range(G):
            for h in range(2):
                first_word = WORDS * 2 * g + WORDS * h
                nc.vector.transpose(
                    out=w_grouped_words[LAST][:, first_word : first_word + WORDS],
                    in_=w_words[LAST][:, first_word : first_word + WORDS],
                )
                quantise_w(LAST, g, HALF * h, HALF)
        acc_last = [
            sums.tile([P, HALF], F32, name="acc_last%d" % h, tag="acc") for h in range(2)
        ]
        for g in range(G):
            for h in range(2):
                passes(acc_last[h], LAST, g, HALF * h, HALF, all_rows)
        blocks_of_half = BLOCK // 2
        for h in range(2):
            (scalar_copy if h == 0 else vector_copy)(
                out=out_sb[LAST][:].rearrange("j (m b) -> j m b", b=BLOCK)[
                    :, :, blocks_of_half * h : blocks_of_half * (h + 1)
                ],
                in_=acc_last[h][:].rearrange("j (b m) -> j m b", m=ROWS_M),
            )
        store(LAST)
